import numpy as np
import ml_dtypes


def mxq(x, axis, fmt="e4m3"):
    dtype, down = {"e4m3": (ml_dtypes.float8_e4m3fn, 7), "e5m2": (ml_dtypes.float8_e5m2, 14)}[fmt]
    v = np.moveaxis(np.asarray(x, np.float32).astype(ml_dtypes.bfloat16).astype(np.float64), axis, -1)
    blocks = v.reshape(v.shape[:-1] + (-1, 32))
    amax = np.abs(blocks).max(-1, keepdims=True)
    byte = np.maximum(np.where(amax > 0, np.frexp(amax)[1] - 1 + 127, 0) - down, 1)
    scale = np.exp2(byte - 127.0)
    codes = (blocks / scale).astype(np.float32).astype(dtype).astype(np.float64)
    return np.moveaxis((codes * scale).reshape(v.shape), -1, axis)


WIDE = False


def mx_kscale(k):
    if not WIDE:
        return np.ones(k)
    levels = np.array([10, -10, 5, -5, 0])
    a = np.random.permutation(np.resize(levels, k // 512 * 4)).reshape(k // 512, 4)
    idx = np.arange(k)
    return np.exp2(a[idx // 512, idx % 128 // 32])


BF16 = ml_dtypes.bfloat16


def bf(x):
    return np.asarray(x, np.float32).astype(BF16)


def f64(x):
    return np.asarray(x).astype(np.float64)


B, T, DIM, H, D = 16, 1024, 128, 4, 128
E = H * D


def softmax(z):
    e = np.exp(z - z.max(-1, keepdims=True))
    return e / e.sum(-1, keepdims=True)


def setup_inputs():
    u = mx_kscale(E).reshape(H, D)
    q = softmax(3.0 * np.random.standard_normal((B, H, T, D)))
    k_sum = (T / D) * np.exp(0.3 * np.random.standard_normal((B, H, 1, D)))
    amp = 2.0 * np.sqrt(T * np.mean(q * q))
    context = k_sum.transpose(0, 1, 3, 2) * 0.2 * np.random.standard_normal((1, H, 1, D)) + amp * np.random.standard_normal((B, H, D, D))
    return {"q": bf(q * u[None, :, None, :]),
            "k_sum": bf(k_sum / u[None, :, None, :]),
            "context": bf(context * u[None, :, None, :] / u[None, :, :, None]),
            "Wp": bf(np.random.standard_normal((DIM, E)) * 2.0 / np.sqrt(E) / u.reshape(E)),
            "bp": bf(np.random.standard_normal(DIM) * 0.2)}


def reference(q, k_sum, context, Wp, bp):
    d_inv = 1.0 / (f64(q) * f64(k_sum)).sum(axis=-1, keepdims=True)
    o = (f64(q) @ f64(context)) * d_inv + f64(q)
    o = o.transpose(0, 2, 1, 3).reshape(B, T, E)
    return (mxq(o, 2, "e4m3") @ mxq(f64(Wp), 1, "e4m3").T) + f64(bp)

@@ -1,0 +1,206 @@
+from contextlib import ExitStack
+
+import concourse.mybir as mybir
+from concourse.masks import make_identity
+
+BF16 = mybir.dt.bfloat16
+F32 = mybir.dt.float32
+U32 = mybir.dt.uint32
+U8 = mybir.dt.uint8
+FP8X4 = mybir.dt.float8_e4m3fn_x4
+MULT = mybir.AluOpType.mult
+ADD = mybir.AluOpType.add
+
+B, H, T, D = 16, 4, 1024, 128
+DIM = 128
+E = H * D
+P = 128
+PACK = 4
+CHUNKS = T // P
+HALF = CHUNKS // 2
+HALVES = 2 * B
+PAIRS = 2 * HALVES
+BANK_F32 = 512
+CTX_PITCH = 144
+CTX_BATCHES = 4
+
+FLOPS = 2 * B * H * T * D * D + 2 * B * T * E * DIM
+
+
+def tile_linearattention_pb_t_kernel(tc, q, k_sum, context, Wp, bp, out):
+    nc = tc.nc
+    with ExitStack() as stack:
+        consts = stack.enter_context(tc.tile_pool(name="consts", bufs=1))
+        q_pool = stack.enter_context(tc.tile_pool(name="q", bufs=HALVES))
+        qT_pool = stack.enter_context(tc.tile_pool(name="qT", bufs=4))
+        dinv_pool = stack.enter_context(tc.tile_pool(name="dinv", bufs=6))
+        om_pool = stack.enter_context(tc.tile_pool(name="om", bufs=3))
+        grouped_pool = stack.enter_context(tc.tile_pool(name="grouped", bufs=3))
+        mx_pool = stack.enter_context(tc.tile_pool(name="mx", bufs=4))
+        out_pool = stack.enter_context(tc.tile_pool(name="out", bufs=8))
+        psum_tq = stack.enter_context(tc.psum_pool(name="psum_tq", bufs=2))
+        psum_prod = stack.enter_context(tc.psum_pool(name="psum_prod", bufs=4))
+        psum_tom = stack.enter_context(tc.psum_pool(name="psum_tom", bufs=1))
+        psum_res = stack.enter_context(tc.psum_pool(name="psum_res", bufs=1))
+        stack.enter_context(tc.manual_schedule())
+
+        ksum_rows = consts.tile([P, D], BF16)
+        nc.vector.memset(ksum_rows[:], 0.0)
+        nc.sync.dma_start(out=ksum_rows[0 : B * H, :], in_=k_sum.rearrange("b h o d -> (b h o) d"))
+        wp_rows = consts.tile([P, E], BF16)
+        bias_bf16 = consts.tile([P, DIM], BF16)
+        ctx_tiles = []
+        q_tiles = []
+        context_by_feature = context.rearrange("b h d e -> d (b h) e")
+        for b in range(B):
+            if b % CTX_BATCHES == 0:
+                ctx = consts.tile([P, CTX_BATCHES * H, CTX_PITCH], BF16, name="ctx%d" % b)
+                heads = slice(b * H, (b + CTX_BATCHES) * H)
+                nc.sync.dma_start(out=ctx[:, :, 0:D], in_=context_by_feature[:, heads, :])
+                ctx_tiles.append(ctx)
+            q_by_token = q[b].rearrange("h (p c) d -> p h c d", c=CHUNKS)
+            for half in range(2):
+                q_half = q_pool.tile([P, H, HALF, D], BF16)
+                nc.sync.dma_start(out=q_half[:], in_=q_by_token[:, :, half * HALF : (half + 1) * HALF, :])
+                q_tiles.append(q_half)
+            if b == 0:
+                nc.sync.dma_start(out=wp_rows[:], in_=Wp)
+                nc.sync.dma_start(out=bias_bf16[:], in_=bp.partition_broadcast(P))
+
+        ident_bf16 = consts.tile([P, P], BF16)
+        make_identity(nc, ident_bf16[:])
+        ident_f32 = consts.tile([P, P], F32)
+        make_identity(nc, ident_f32[:])
+
+        ksum_ps = psum_tq.tile([P, 2, H, P], BF16, tag="tq")
+        nc.tensor.transpose(ksum_ps[:, 0, 0, :], ksum_rows[:], ident_bf16[:])
+        for g in range(B // CTX_BATCHES):
+            heads = slice(g * CTX_BATCHES * H, (g + 1) * CTX_BATCHES * H)
+            nc.vector.tensor_copy(out=ctx_tiles[g][:, :, D], in_=ksum_ps[:, 0, 0, heads])
+
+        wp_ps = psum_tom.tile([P, 2, 2, P], F32, tag="tom")
+        wp_words = wp_rows[:].bitcast(F32)
+        for u in range(2):
+            nc.tensor.transpose(wp_ps[:, 0, u, :], wp_words[:, u * P : (u + 1) * P], ident_f32[:])
+        wp_grouped = consts.tile([P, DIM * PACK], BF16, align_bytes=64)
+        nc.vector.tensor_copy(
+            out=wp_grouped[:].bitcast(F32).rearrange("p (n u) -> p n u", u=2),
+            in_=wp_ps[:, 0, :, :].rearrange("p u n -> p n u"),
+        )
+        bias = consts.tile([P, DIM], F32)
+        nc.vector.tensor_copy(out=bias[:], in_=bias_bf16[:])
+        wp_codes = consts.tile([P, DIM], U32, align_bytes=64)
+        wp_scales = consts.tile([P, DIM], U8, align_bytes=64)
+        nc.vector.quantize_mx(out=wp_codes[:].bitcast(FP8X4), scales=wp_scales[:], in_=wp_grouped[:])
+
+        qT_tiles = {}
+        om_tiles = {}
+        grouped_tiles = {}
+        mx_tiles = {}
+
+        def chunk_in_half(pair, cc):
+            return 2 * (pair % 2) + cc
+
+        def transpose_queries(pair):
+            q_half = q_tiles[pair // 2]
+            tq = psum_tq.tile([P, 2, H, P], BF16, tag="tq")
+            for cc in range(2):
+                for h in range(H):
+                    nc.tensor.transpose(tq[:, cc, h, :], q_half[:, h, chunk_in_half(pair, cc), :], ident_bf16[:])
+            qT = qT_pool.tile([P, 2, H, P], BF16)
+            nc.scalar.copy(out=qT[:], in_=tq[:])
+            qT_tiles[pair] = qT
+
+        def attend(pair, cc, head_pair):
+            b = pair // (CHUNKS // 2)
+            prod = psum_prod.tile([P, 2, BANK_F32 // 2], F32)
+            for j in range(2):
+                h = 2 * head_pair + j
+                nc.tensor.matmul(
+                    out=prod[:, j, 0 : D + 1],
+                    lhsT=qT_tiles[pair][:, cc, h, :],
+                    rhs=ctx_tiles[b // CTX_BATCHES][:, (b % CTX_BATCHES) * H + h, 0 : D + 1],
+                    start=True,
+                    stop=True,
+                )
+            d_inv = dinv_pool.tile([P, 2], F32)
+            nc.vector.reciprocal(out=d_inv[:], in_=prod[:, :, D])
+            return pair, cc, head_pair, prod, d_inv
+
+        def normalise(pair, cc, head_pair, prod, d_inv):
+            if cc == 0 and head_pair == 0:
+                om_new = om_pool.tile([P, 2, E], BF16)
+                om_tiles[pair] = om_new
+            for j in range(2):
+                h = 2 * head_pair + j
+                nc.vector.scalar_tensor_tensor(
+                    out=om_tiles[pair][:, cc, h * D : (h + 1) * D],
+                    in0=prod[:, j, 0:D],
+                    scalar=d_inv[:, j : j + 1],
+                    in1=q_tiles[pair // 2][:, h, chunk_in_half(pair, cc), :],
+                    op0=MULT,
+                    op1=ADD,
+                )
+
+        def transpose_outputs(pair):
+            om_words = om_tiles[pair][:].bitcast(F32)
+            tom = psum_tom.tile([P, 2, 2, P], F32, tag="tom")
+            for cc in range(2):
+                for u in range(2):
+                    nc.tensor.transpose(tom[:, cc, u, :], om_words[:, cc, u * P : (u + 1) * P], ident_f32[:])
+            grouped = grouped_pool.tile([P, 2 * P * PACK], BF16, align_bytes=64)
+            nc.scalar.copy(
+                out=grouped[:].bitcast(F32).rearrange("p (c t u) -> p c t u", c=2, u=2),
+                in_=tom[:].rearrange("p c u t -> p c t u"),
+            )
+            grouped_tiles[pair] = grouped
+
+        def quantise(pair):
+            if pair % 2 == 0:
+                codes_new = mx_pool.tile([P, HALF * P], U32, align_bytes=64)
+                scales_new = mx_pool.tile([P, HALF * P], U8, align_bytes=64)
+                mx_tiles[pair // 2] = (codes_new, scales_new)
+            codes, scales = mx_tiles[pair // 2]
+            cols = slice((pair % 2) * 2 * P, (pair % 2 + 1) * 2 * P)
+            nc.vector.quantize_mx(out=codes[:, cols].bitcast(FP8X4), scales=scales[:, cols], in_=grouped_tiles[pair][:])
+
+        def project(half_batch):
+            codes, scales = mx_tiles[half_batch]
+            res = psum_res.tile([P, HALF, DIM], F32)
+            for c in range(HALF):
+                tokens = slice(c * P, (c + 1) * P)
+                nc.tensor.matmul_mx(
+                    out=res[:, c, :],
+                    lhsT=codes[:, tokens].bitcast(FP8X4),
+                    lhsT_scale=scales[:, tokens],
+                    rhs=wp_codes[:].bitcast(FP8X4),
+                    rhs_scale=wp_scales[:],
+                    start=True,
+                    stop=True,
+                )
+            out_sb = out_pool.tile([P, HALF, DIM], F32)
+            nc.scalar.copy(out=out_sb[:], in_=res[:])
+            nc.gpsimd.tensor_tensor(
+                out=out_sb[:], in0=out_sb[:], in1=bias[:].unsqueeze(1).to_broadcast([P, HALF, DIM]), op=ADD
+            )
+            b, half = divmod(half_batch, 2)
+            out_by_token = out[b].rearrange("(p c) n -> p c n", c=CHUNKS)
+            nc.sync.dma_start(out=out_by_token[:, half * HALF : (half + 1) * HALF, :], in_=out_sb[:])
+
+        transpose_queries(0)
+        transpose_queries(1)
+        waiting = None
+        for r in range(PAIRS + 3):
+            for bank in range(4):
+                if bank == 2 and r % 2 == 0 and 0 <= (r - 4) // 2 < HALVES:
+                    project((r - 4) // 2)
+                filled = attend(r, bank // 2, bank % 2) if r < PAIRS else None
+                if waiting is not None:
+                    normalise(*waiting)
+                waiting = filled
+            if 0 <= r - 1 < PAIRS:
+                transpose_outputs(r - 1)
+            if r + 2 < PAIRS:
+                transpose_queries(r + 2)
+            if 0 <= r - 2 < PAIRS:
+                quantise(r - 2)

@@ -20,9 +20,11 @@ CHUNKS = T // P
 HALF = CHUNKS // 2
 HALVES = 2 * B
 PAIRS = 2 * HALVES
+PSUM_BANKS = 8
 BANK_F32 = 512
+BANKS_PER_PAIR = 4
 CTX_PITCH = 144
-CTX_BATCHES = 4
+PROJECT_LAG = 5
 
 FLOPS = 2 * B * H * T * D * D + 2 * B * T * E * DIM
 
@@ -33,15 +35,12 @@ def tile_linearattention_pb_t_kernel(tc, q, k_sum, context, Wp, bp, out):
         consts = stack.enter_context(tc.tile_pool(name="consts", bufs=1))
         q_pool = stack.enter_context(tc.tile_pool(name="q", bufs=HALVES))
         qT_pool = stack.enter_context(tc.tile_pool(name="qT", bufs=4))
-        dinv_pool = stack.enter_context(tc.tile_pool(name="dinv", bufs=6))
-        om_pool = stack.enter_context(tc.tile_pool(name="om", bufs=3))
+        dinv_pool = stack.enter_context(tc.tile_pool(name="dinv", bufs=8))
+        om_pool = stack.enter_context(tc.tile_pool(name="om", bufs=4))
         grouped_pool = stack.enter_context(tc.tile_pool(name="grouped", bufs=3))
-        mx_pool = stack.enter_context(tc.tile_pool(name="mx", bufs=4))
+        mx_pool = stack.enter_context(tc.tile_pool(name="mx", bufs=5))
         out_pool = stack.enter_context(tc.tile_pool(name="out", bufs=8))
-        psum_tq = stack.enter_context(tc.psum_pool(name="psum_tq", bufs=2))
-        psum_prod = stack.enter_context(tc.psum_pool(name="psum_prod", bufs=4))
-        psum_tom = stack.enter_context(tc.psum_pool(name="psum_tom", bufs=1))
-        psum_res = stack.enter_context(tc.psum_pool(name="psum_res", bufs=1))
+        psum = stack.enter_context(tc.psum_pool(name="psum", bufs=PSUM_BANKS))
         stack.enter_context(tc.manual_schedule())
 
         ksum_rows = consts.tile([P, D], BF16)
@@ -49,20 +48,18 @@ def tile_linearattention_pb_t_kernel(tc, q, k_sum, context, Wp, bp, out):
         nc.sync.dma_start(out=ksum_rows[0 : B * H, :], in_=k_sum.rearrange("b h o d -> (b h o) d"))
         wp_rows = consts.tile([P, E], BF16)
         bias_bf16 = consts.tile([P, DIM], BF16)
-        ctx_tiles = []
+        ctx = consts.tile([P, B * H, CTX_PITCH], BF16)
         q_tiles = []
         context_by_feature = context.rearrange("b h d e -> d (b h) e")
         for b in range(B):
-            if b % CTX_BATCHES == 0:
-                ctx = consts.tile([P, CTX_BATCHES * H, CTX_PITCH], BF16, name="ctx%d" % b)
-                heads = slice(b * H, (b + CTX_BATCHES) * H)
-                nc.sync.dma_start(out=ctx[:, :, 0:D], in_=context_by_feature[:, heads, :])
-                ctx_tiles.append(ctx)
             q_by_token = q[b].rearrange("h (p c) d -> p h c d", c=CHUNKS)
             for half in range(2):
                 q_half = q_pool.tile([P, H, HALF, D], BF16)
                 nc.sync.dma_start(out=q_half[:], in_=q_by_token[:, :, half * HALF : (half + 1) * HALF, :])
                 q_tiles.append(q_half)
+                if half == 0:
+                    heads = slice(b * H, (b + 1) * H)
+                    nc.sync.dma_start(out=ctx[:, heads, 0:D], in_=context_by_feature[:, heads, :])
             if b == 0:
                 nc.sync.dma_start(out=wp_rows[:], in_=Wp)
                 nc.sync.dma_start(out=bias_bf16[:], in_=bp.partition_broadcast(P))
@@ -72,27 +69,11 @@ def tile_linearattention_pb_t_kernel(tc, q, k_sum, context, Wp, bp, out):
         ident_f32 = consts.tile([P, P], F32)
         make_identity(nc, ident_f32[:])
 
-        ksum_ps = psum_tq.tile([P, 2, H, P], BF16, tag="tq")
+        ksum_ps = psum.tile([P, 2, H, P], BF16, tag="bank")
         nc.tensor.transpose(ksum_ps[:, 0, 0, :], ksum_rows[:], ident_bf16[:])
-        for g in range(B // CTX_BATCHES):
-            heads = slice(g * CTX_BATCHES * H, (g + 1) * CTX_BATCHES * H)
-            nc.vector.tensor_copy(out=ctx_tiles[g][:, :, D], in_=ksum_ps[:, 0, 0, heads])
+        nc.vector.tensor_copy(out=ctx[:, :, D], in_=ksum_ps[:, 0, 0, 0 : B * H])
 
-        wp_ps = psum_tom.tile([P, 2, 2, P], F32, tag="tom")
-        wp_words = wp_rows[:].bitcast(F32)
-        for u in range(2):
-            nc.tensor.transpose(wp_ps[:, 0, u, :], wp_words[:, u * P : (u + 1) * P], ident_f32[:])
-        wp_grouped = consts.tile([P, DIM * PACK], BF16, align_bytes=64)
-        nc.vector.tensor_copy(
-            out=wp_grouped[:].bitcast(F32).rearrange("p (n u) -> p n u", u=2),
-            in_=wp_ps[:, 0, :, :].rearrange("p u n -> p n u"),
-        )
-        bias = consts.tile([P, DIM], F32)
-        nc.vector.tensor_copy(out=bias[:], in_=bias_bf16[:])
-        wp_codes = consts.tile([P, DIM], U32, align_bytes=64)
-        wp_scales = consts.tile([P, DIM], U8, align_bytes=64)
-        nc.vector.quantize_mx(out=wp_codes[:].bitcast(FP8X4), scales=wp_scales[:], in_=wp_grouped[:])
-
+        tq_tiles = {}
         qT_tiles = {}
         om_tiles = {}
         grouped_tiles = {}
@@ -101,50 +82,57 @@ def tile_linearattention_pb_t_kernel(tc, q, k_sum, context, Wp, bp, out):
         def chunk_in_half(pair, cc):
             return 2 * (pair % 2) + cc
 
-        def transpose_queries(pair):
-            q_half = q_tiles[pair // 2]
-            tq = psum_tq.tile([P, 2, H, P], BF16, tag="tq")
-            for cc in range(2):
-                for h in range(H):
-                    nc.tensor.transpose(tq[:, cc, h, :], q_half[:, h, chunk_in_half(pair, cc), :], ident_bf16[:])
-            qT = qT_pool.tile([P, 2, H, P], BF16)
-            nc.scalar.copy(out=qT[:], in_=tq[:])
-            qT_tiles[pair] = qT
+        def transpose_queries(pair, quarter):
+            if quarter == 0:
+                tq_new = psum.tile([P, 2, H, P], BF16, tag="bank")
+                tq_tiles[pair] = tq_new
+            tq = tq_tiles[pair]
+            for block in (2 * quarter, 2 * quarter + 1):
+                cc, h = divmod(block, H)
+                nc.tensor.transpose(tq[:, cc, h, :], q_tiles[pair // 2][:, h, chunk_in_half(pair, cc), :], ident_bf16[:])
+            if quarter == BANKS_PER_PAIR - 1:
+                qT = qT_pool.tile([P, 2, H, P], BF16)
+                nc.scalar.copy(out=qT[:], in_=tq[:])
+                qT_tiles[pair] = qT
 
-        def attend(pair, cc, head_pair):
+        def multiply(pair, bank):
             b = pair // (CHUNKS // 2)
-            prod = psum_prod.tile([P, 2, BANK_F32 // 2], F32)
+            cc, head_pair = divmod(bank, 2)
+            prod = psum.tile([P, 2, BANK_F32 // 2], F32, tag="bank")
             for j in range(2):
                 h = 2 * head_pair + j
                 nc.tensor.matmul(
                     out=prod[:, j, 0 : D + 1],
                     lhsT=qT_tiles[pair][:, cc, h, :],
-                    rhs=ctx_tiles[b // CTX_BATCHES][:, (b % CTX_BATCHES) * H + h, 0 : D + 1],
+                    rhs=ctx[:, b * H + h, 0 : D + 1],
                     start=True,
                     stop=True,
                 )
             d_inv = dinv_pool.tile([P, 2], F32)
-            nc.vector.reciprocal(out=d_inv[:], in_=prod[:, :, D])
             return pair, cc, head_pair, prod, d_inv
 
-        def normalise(pair, cc, head_pair, prod, d_inv):
-            if cc == 0 and head_pair == 0:
+        def invert(filled_bank):
+            prod, d_inv = filled_bank[3], filled_bank[4]
+            nc.vector.reciprocal(out=d_inv[:], in_=prod[:, :, D])
+
+        def normalise(filled_bank, j):
+            pair, cc, head_pair, prod, d_inv = filled_bank
+            if cc == 0 and head_pair == 0 and j == 0:
                 om_new = om_pool.tile([P, 2, E], BF16)
                 om_tiles[pair] = om_new
-            for j in range(2):
-                h = 2 * head_pair + j
-                nc.vector.scalar_tensor_tensor(
-                    out=om_tiles[pair][:, cc, h * D : (h + 1) * D],
-                    in0=prod[:, j, 0:D],
-                    scalar=d_inv[:, j : j + 1],
-                    in1=q_tiles[pair // 2][:, h, chunk_in_half(pair, cc), :],
-                    op0=MULT,
-                    op1=ADD,
-                )
+            h = 2 * head_pair + j
+            nc.vector.scalar_tensor_tensor(
+                out=om_tiles[pair][:, cc, h * D : (h + 1) * D],
+                in0=prod[:, j, 0:D],
+                scalar=d_inv[:, j : j + 1],
+                in1=q_tiles[pair // 2][:, h, chunk_in_half(pair, cc), :],
+                op0=MULT,
+                op1=ADD,
+            )
 
         def transpose_outputs(pair):
             om_words = om_tiles[pair][:].bitcast(F32)
-            tom = psum_tom.tile([P, 2, 2, P], F32, tag="tom")
+            tom = psum.tile([P, 2, 2, P], F32, tag="bank")
             for cc in range(2):
                 for u in range(2):
                     nc.tensor.transpose(tom[:, cc, u, :], om_words[:, cc, u * P : (u + 1) * P], ident_f32[:])
@@ -166,7 +154,7 @@ def tile_linearattention_pb_t_kernel(tc, q, k_sum, context, Wp, bp, out):
 
         def project(half_batch):
             codes, scales = mx_tiles[half_batch]
-            res = psum_res.tile([P, HALF, DIM], F32)
+            res = psum.tile([P, HALF, DIM], F32, tag="bank")
             for c in range(HALF):
                 tokens = slice(c * P, (c + 1) * P)
                 nc.tensor.matmul_mx(
@@ -187,20 +175,48 @@ def tile_linearattention_pb_t_kernel(tc, q, k_sum, context, Wp, bp, out):
             out_by_token = out[b].rearrange("(p c) n -> p c n", c=CHUNKS)
             nc.sync.dma_start(out=out_by_token[:, half * HALF : (half + 1) * HALF, :], in_=out_sb[:])
 
-        transpose_queries(0)
-        transpose_queries(1)
-        waiting = None
-        for r in range(PAIRS + 3):
-            for bank in range(4):
-                if bank == 2 and r % 2 == 0 and 0 <= (r - 4) // 2 < HALVES:
-                    project((r - 4) // 2)
-                filled = attend(r, bank // 2, bank % 2) if r < PAIRS else None
+        for pair in range(2):
+            for quarter in range(BANKS_PER_PAIR):
+                transpose_queries(pair, quarter)
+
+        def run_round(r, waiting):
+            for bank in range(BANKS_PER_PAIR):
+                if bank == 2 and (r - PROJECT_LAG) % 2 == 0 and 0 <= r - PROJECT_LAG < PAIRS:
+                    project((r - PROJECT_LAG) // 2)
+                filled = multiply(r, bank) if r < PAIRS else None
                 if waiting is not None:
-                    normalise(*waiting)
+                    normalise(waiting, 0)
+                if filled is not None:
+                    invert(filled)
+                if waiting is not None:
+                    normalise(waiting, 1)
                 waiting = filled
+                if r + 2 < PAIRS:
+                    transpose_queries(r + 2, bank)
             if 0 <= r - 1 < PAIRS:
                 transpose_outputs(r - 1)
-            if r + 2 < PAIRS:
-                transpose_queries(r + 2)
             if 0 <= r - 2 < PAIRS:
                 quantise(r - 2)
+            return waiting
+
+        waiting = None
+        for r in range(2):
+            waiting = run_round(r, waiting)
+
+        wp_ps = psum.tile([P, 2, 2, P], F32, tag="bank")
+        wp_words = wp_rows[:].bitcast(F32)
+        for u in range(2):
+            nc.tensor.transpose(wp_ps[:, 0, u, :], wp_words[:, u * P : (u + 1) * P], ident_f32[:])
+        wp_grouped = consts.tile([P, DIM * PACK], BF16, align_bytes=64)
+        nc.vector.tensor_copy(
+            out=wp_grouped[:].bitcast(F32).rearrange("p (n u) -> p n u", u=2),
+            in_=wp_ps[:, 0, :, :].rearrange("p u n -> p n u"),
+        )
+        bias = consts.tile([P, DIM], F32)
+        nc.vector.tensor_copy(out=bias[:], in_=bias_bf16[:])
+        wp_codes = consts.tile([P, DIM], U32, align_bytes=64)
+        wp_scales = consts.tile([P, DIM], U8, align_bytes=64)
+        nc.vector.quantize_mx(out=wp_codes[:].bitcast(FP8X4), scales=wp_scales[:], in_=wp_grouped[:])
+
+        for r in range(2, PAIRS + PROJECT_LAG - 1):
+            waiting = run_round(r, waiting)

@@ -167,9 +167,8 @@ def tile_linearattention_pb_t_kernel(tc, q, k_sum, context, Wp, bp, out):
                     stop=True,
                 )
             out_sb = out_pool.tile([P, HALF, DIM], F32)
-            nc.scalar.copy(out=out_sb[:], in_=res[:])
-            nc.gpsimd.tensor_tensor(
-                out=out_sb[:], in0=out_sb[:], in1=bias[:].unsqueeze(1).to_broadcast([P, HALF, DIM]), op=ADD
+            nc.vector.tensor_tensor(
+                out=out_sb[:], in0=res[:], in1=bias[:].unsqueeze(1).to_broadcast([P, HALF, DIM]), op=ADD
             )
             b, half = divmod(half_batch, 2)
             out_by_token = out[b].rearrange("(p c) n -> p c n", c=CHUNKS)

@@ -8,6 +8,7 @@ F32 = mybir.dt.float32
 U32 = mybir.dt.uint32
 U8 = mybir.dt.uint8
 FP8X4 = mybir.dt.float8_e4m3fn_x4
+IDENTITY = mybir.ActivationFunctionType.Identity
 MULT = mybir.AluOpType.mult
 ADD = mybir.AluOpType.add
 
@@ -39,15 +40,16 @@ def tile_linearattention_pb_t_kernel(tc, q, k_sum, context, Wp, bp, out):
         om_pool = stack.enter_context(tc.tile_pool(name="om", bufs=4))
         grouped_pool = stack.enter_context(tc.tile_pool(name="grouped", bufs=3))
         mx_pool = stack.enter_context(tc.tile_pool(name="mx", bufs=5))
+        resT_pool = stack.enter_context(tc.tile_pool(name="resT", bufs=3))
         out_pool = stack.enter_context(tc.tile_pool(name="out", bufs=8))
         psum = stack.enter_context(tc.psum_pool(name="psum", bufs=PSUM_BANKS))
         stack.enter_context(tc.manual_schedule())
 
-        ksum_rows = consts.tile([P, D], BF16)
-        nc.vector.memset(ksum_rows[:], 0.0)
-        nc.sync.dma_start(out=ksum_rows[0 : B * H, :], in_=k_sum.rearrange("b h o d -> (b h o) d"))
+        small_rows = consts.tile([P, D], BF16)
+        nc.vector.memset(small_rows[:], 0.0)
+        nc.sync.dma_start(out=small_rows[0 : B * H, :], in_=k_sum.rearrange("b h o d -> (b h o) d"))
+        nc.sync.dma_start(out=small_rows[B * H : B * H + 1, :], in_=bp.rearrange("(o n) -> o n", o=1))
         wp_rows = consts.tile([P, E], BF16)
-        bias_bf16 = consts.tile([P, DIM], BF16)
         ctx = consts.tile([P, B * H, CTX_PITCH], BF16)
         q_tiles = []
         context_by_feature = context.rearrange("b h d e -> d (b h) e")
@@ -62,22 +64,24 @@ def tile_linearattention_pb_t_kernel(tc, q, k_sum, context, Wp, bp, out):
                     nc.sync.dma_start(out=ctx[:, heads, 0:D], in_=context_by_feature[:, heads, :])
             if b == 0:
                 nc.sync.dma_start(out=wp_rows[:], in_=Wp)
-                nc.sync.dma_start(out=bias_bf16[:], in_=bp.partition_broadcast(P))
 
         ident_bf16 = consts.tile([P, P], BF16)
         make_identity(nc, ident_bf16[:])
         ident_f32 = consts.tile([P, P], F32)
         make_identity(nc, ident_f32[:])
 
-        ksum_ps = psum.tile([P, 2, H, P], BF16, tag="bank")
-        nc.tensor.transpose(ksum_ps[:, 0, 0, :], ksum_rows[:], ident_bf16[:])
-        nc.vector.tensor_copy(out=ctx[:, :, D], in_=ksum_ps[:, 0, 0, 0 : B * H])
+        small_ps = psum.tile([P, 2, H, P], BF16, tag="bank")
+        nc.tensor.transpose(small_ps[:, 0, 0, :], small_rows[:], ident_bf16[:])
+        nc.vector.tensor_copy(out=ctx[:, :, D], in_=small_ps[:, 0, 0, 0 : B * H])
+        bias = consts.tile([P, 1], F32)
+        nc.vector.tensor_copy(out=bias[:], in_=small_ps[:, 0, 0, B * H : B * H + 1])
 
         tq_tiles = {}
         qT_tiles = {}
         om_tiles = {}
         grouped_tiles = {}
         mx_tiles = {}
+        resT_tiles = {}
 
         def chunk_in_half(pair, cc):
             return 2 * (pair % 2) + cc
@@ -154,22 +158,26 @@ def tile_linearattention_pb_t_kernel(tc, q, k_sum, context, Wp, bp, out):
 
         def project(half_batch):
             codes, scales = mx_tiles[half_batch]
+            resT = psum.tile([P, HALF * P], F32, tag="bank")
+            nc.tensor.matmul_mx(
+                out=resT[:],
+                lhsT=wp_codes[:].bitcast(FP8X4),
+                lhsT_scale=wp_scales[:],
+                rhs=codes[:].bitcast(FP8X4),
+                rhs_scale=scales[:],
+                start=True,
+                stop=True,
+            )
+            resT_sb = resT_pool.tile([P, HALF * P], F32)
+            nc.scalar.activation(out=resT_sb[:], in_=resT[:], func=IDENTITY, bias=bias[:, 0:1], scale=1.0)
+            resT_tiles[half_batch] = resT_sb
+
+        def store(half_batch):
             res = psum.tile([P, HALF, DIM], F32, tag="bank")
             for c in range(HALF):
-                tokens = slice(c * P, (c + 1) * P)
-                nc.tensor.matmul_mx(
-                    out=res[:, c, :],
-                    lhsT=codes[:, tokens].bitcast(FP8X4),
-                    lhsT_scale=scales[:, tokens],
-                    rhs=wp_codes[:].bitcast(FP8X4),
-                    rhs_scale=wp_scales[:],
-                    start=True,
-                    stop=True,
-                )
+                nc.tensor.transpose(res[:, c, :], resT_tiles[half_batch][:, c * P : (c + 1) * P], ident_f32[:])
             out_sb = out_pool.tile([P, HALF, DIM], F32)
-            nc.vector.tensor_tensor(
-                out=out_sb[:], in0=res[:], in1=bias[:].unsqueeze(1).to_broadcast([P, HALF, DIM]), op=ADD
-            )
+            nc.scalar.copy(out=out_sb[:], in_=res[:])
             b, half = divmod(half_batch, 2)
             out_by_token = out[b].rearrange("(p c) n -> p c n", c=CHUNKS)
             nc.sync.dma_start(out=out_by_token[:, half * HALF : (half + 1) * HALF, :], in_=out_sb[:])
@@ -182,6 +190,8 @@ def tile_linearattention_pb_t_kernel(tc, q, k_sum, context, Wp, bp, out):
             for bank in range(BANKS_PER_PAIR):
                 if bank == 2 and (r - PROJECT_LAG) % 2 == 0 and 0 <= r - PROJECT_LAG < PAIRS:
                     project((r - PROJECT_LAG) // 2)
+                if bank == 2 and (r - PROJECT_LAG) % 2 == 1 and 0 <= r - PROJECT_LAG - 1 < PAIRS:
+                    store((r - PROJECT_LAG - 1) // 2)
                 filled = multiply(r, bank) if r < PAIRS else None
                 if waiting is not None:
                     normalise(waiting, 0)
@@ -211,11 +221,9 @@ def tile_linearattention_pb_t_kernel(tc, q, k_sum, context, Wp, bp, out):
             out=wp_grouped[:].bitcast(F32).rearrange("p (n u) -> p n u", u=2),
             in_=wp_ps[:, 0, :, :].rearrange("p u n -> p n u"),
         )
-        bias = consts.tile([P, DIM], F32)
-        nc.vector.tensor_copy(out=bias[:], in_=bias_bf16[:])
         wp_codes = consts.tile([P, DIM], U32, align_bytes=64)
         wp_scales = consts.tile([P, DIM], U8, align_bytes=64)
         nc.vector.quantize_mx(out=wp_codes[:].bitcast(FP8X4), scales=wp_scales[:], in_=wp_grouped[:])
 
-        for r in range(2, PAIRS + PROJECT_LAG - 1):
+        for r in range(2, PAIRS + PROJECT_LAG):
             waiting = run_round(r, waiting)

@@ -22,12 +22,18 @@ HALF = CHUNKS // 2
 HALVES = 2 * B
 PAIRS = 2 * HALVES
 PSUM_BANKS = 8
-BANK_F32 = 512
-BANKS_PER_PAIR = 4
-CTX_PITCH = 144
+QUANTISE_LAG = 3
 PROJECT_LAG = 5
+STORE_LAG = 6
 
 FLOPS = 2 * B * H * T * D * D + 2 * B * T * E * DIM
+
+
+def half_batch_due(r, lag):
+    first_round = r - lag
+    if first_round % 2 == 0 and 0 <= first_round < PAIRS:
+        return first_round // 2
+    return None
 
 
 def tile_linearattention_pb_t_kernel(tc, q, k_sum, context, Wp, bp, out):
@@ -36,10 +42,10 @@ def tile_linearattention_pb_t_kernel(tc, q, k_sum, context, Wp, bp, out):
         consts = stack.enter_context(tc.tile_pool(name="consts", bufs=1))
         q_pool = stack.enter_context(tc.tile_pool(name="q", bufs=HALVES))
         qT_pool = stack.enter_context(tc.tile_pool(name="qT", bufs=4))
-        dinv_pool = stack.enter_context(tc.tile_pool(name="dinv", bufs=8))
+        dinv_pool = stack.enter_context(tc.tile_pool(name="dinv", bufs=4))
         om_pool = stack.enter_context(tc.tile_pool(name="om", bufs=4))
         grouped_pool = stack.enter_context(tc.tile_pool(name="grouped", bufs=3))
-        mx_pool = stack.enter_context(tc.tile_pool(name="mx", bufs=5))
+        mx_pool = stack.enter_context(tc.tile_pool(name="mx", bufs=3))
         resT_pool = stack.enter_context(tc.tile_pool(name="resT", bufs=3))
         out_pool = stack.enter_context(tc.tile_pool(name="out", bufs=8))
         psum = stack.enter_context(tc.psum_pool(name="psum", bufs=PSUM_BANKS))
@@ -50,7 +56,7 @@ def tile_linearattention_pb_t_kernel(tc, q, k_sum, context, Wp, bp, out):
         nc.sync.dma_start(out=small_rows[0 : B * H, :], in_=k_sum.rearrange("b h o d -> (b h o) d"))
         nc.sync.dma_start(out=small_rows[B * H : B * H + 1, :], in_=bp.rearrange("(o n) -> o n", o=1))
         wp_rows = consts.tile([P, E], BF16)
-        ctx = consts.tile([P, B * H, CTX_PITCH], BF16)
+        ctx = consts.tile([P, B * H, D], BF16)
         q_tiles = []
         context_by_feature = context.rearrange("b h d e -> d (b h) e")
         for b in range(B):
@@ -61,7 +67,7 @@ def tile_linearattention_pb_t_kernel(tc, q, k_sum, context, Wp, bp, out):
                 q_tiles.append(q_half)
                 if half == 0:
                     heads = slice(b * H, (b + 1) * H)
-                    nc.sync.dma_start(out=ctx[:, heads, 0:D], in_=context_by_feature[:, heads, :])
+                    nc.sync.dma_start(out=ctx[:, heads, :], in_=context_by_feature[:, heads, :])
             if b == 0:
                 nc.sync.dma_start(out=wp_rows[:], in_=Wp)
 
@@ -70,14 +76,16 @@ def tile_linearattention_pb_t_kernel(tc, q, k_sum, context, Wp, bp, out):
         ident_f32 = consts.tile([P, P], F32)
         make_identity(nc, ident_f32[:])
 
-        small_ps = psum.tile([P, 2, H, P], BF16, tag="bank")
-        nc.tensor.transpose(small_ps[:, 0, 0, :], small_rows[:], ident_bf16[:])
-        nc.vector.tensor_copy(out=ctx[:, :, D], in_=small_ps[:, 0, 0, 0 : B * H])
+        small_ps = psum.tile([P, P], BF16, tag="bank")
+        nc.tensor.transpose(small_ps[:], small_rows[:], ident_bf16[:])
+        ksumT = consts.tile([P, B * H], BF16)
+        nc.vector.tensor_copy(out=ksumT[:], in_=small_ps[:, 0 : B * H])
         bias = consts.tile([P, 1], F32)
-        nc.vector.tensor_copy(out=bias[:], in_=small_ps[:, 0, 0, B * H : B * H + 1])
+        nc.vector.tensor_copy(out=bias[:], in_=small_ps[:, B * H : B * H + 1])
 
         tq_tiles = {}
         qT_tiles = {}
+        dinv_tiles = {}
         om_tiles = {}
         grouped_tiles = {}
         mx_tiles = {}
@@ -86,53 +94,53 @@ def tile_linearattention_pb_t_kernel(tc, q, k_sum, context, Wp, bp, out):
         def chunk_in_half(pair, cc):
             return 2 * (pair % 2) + cc
 
-        def transpose_queries(pair, quarter):
-            if quarter == 0:
+        def transpose_queries(pair, cc):
+            if cc == 0:
                 tq_new = psum.tile([P, 2, H, P], BF16, tag="bank")
                 tq_tiles[pair] = tq_new
             tq = tq_tiles[pair]
-            for block in (2 * quarter, 2 * quarter + 1):
-                cc, h = divmod(block, H)
+            for h in range(H):
                 nc.tensor.transpose(tq[:, cc, h, :], q_tiles[pair // 2][:, h, chunk_in_half(pair, cc), :], ident_bf16[:])
-            if quarter == BANKS_PER_PAIR - 1:
+            if cc == 1:
                 qT = qT_pool.tile([P, 2, H, P], BF16)
                 nc.scalar.copy(out=qT[:], in_=tq[:])
                 qT_tiles[pair] = qT
 
-        def multiply(pair, bank):
+        def denominators(pair):
             b = pair // (CHUNKS // 2)
-            cc, head_pair = divmod(bank, 2)
-            prod = psum.tile([P, 2, BANK_F32 // 2], F32, tag="bank")
-            for j in range(2):
-                h = 2 * head_pair + j
+            den = psum.tile([P, 2, H], F32, tag="bank")
+            for cc in range(2):
+                for h in range(H):
+                    nc.tensor.matmul(
+                        out=den[:, cc, h : h + 1],
+                        lhsT=qT_tiles[pair][:, cc, h, :],
+                        rhs=ksumT[:, b * H + h : b * H + h + 1],
+                        start=True,
+                        stop=True,
+                    )
+            d_inv = dinv_pool.tile([P, 2, H], F32)
+            nc.vector.reciprocal(out=d_inv[:], in_=den[:])
+            dinv_tiles[pair] = d_inv
+
+        def attend(pair, cc):
+            b = pair // (CHUNKS // 2)
+            prod = psum.tile([P, H, D], F32, tag="bank")
+            for h in range(H):
                 nc.tensor.matmul(
-                    out=prod[:, j, 0 : D + 1],
-                    lhsT=qT_tiles[pair][:, cc, h, :],
-                    rhs=ctx[:, b * H + h, 0 : D + 1],
-                    start=True,
-                    stop=True,
+                    out=prod[:, h, :], lhsT=qT_tiles[pair][:, cc, h, :], rhs=ctx[:, b * H + h, :], start=True, stop=True
                 )
-            d_inv = dinv_pool.tile([P, 2], F32)
-            return pair, cc, head_pair, prod, d_inv
-
-        def invert(filled_bank):
-            prod, d_inv = filled_bank[3], filled_bank[4]
-            nc.vector.reciprocal(out=d_inv[:], in_=prod[:, :, D])
-
-        def normalise(filled_bank, j):
-            pair, cc, head_pair, prod, d_inv = filled_bank
-            if cc == 0 and head_pair == 0 and j == 0:
+            if cc == 0:
                 om_new = om_pool.tile([P, 2, E], BF16)
                 om_tiles[pair] = om_new
-            h = 2 * head_pair + j
-            nc.vector.scalar_tensor_tensor(
-                out=om_tiles[pair][:, cc, h * D : (h + 1) * D],
-                in0=prod[:, j, 0:D],
-                scalar=d_inv[:, j : j + 1],
-                in1=q_tiles[pair // 2][:, h, chunk_in_half(pair, cc), :],
-                op0=MULT,
-                op1=ADD,
-            )
+            for h in range(H):
+                nc.vector.scalar_tensor_tensor(
+                    out=om_tiles[pair][:, cc, h * D : (h + 1) * D],
+                    in0=prod[:, h, :],
+                    scalar=dinv_tiles[pair][:, cc, h : h + 1],
+                    in1=q_tiles[pair // 2][:, h, chunk_in_half(pair, cc), :],
+                    op0=MULT,
+                    op1=ADD,
+                )
 
         def transpose_outputs(pair):
             om_words = om_tiles[pair][:].bitcast(F32)
@@ -140,21 +148,18 @@ def tile_linearattention_pb_t_kernel(tc, q, k_sum, context, Wp, bp, out):
             for cc in range(2):
                 for u in range(2):
                     nc.tensor.transpose(tom[:, cc, u, :], om_words[:, cc, u * P : (u + 1) * P], ident_f32[:])
-            grouped = grouped_pool.tile([P, 2 * P * PACK], BF16, align_bytes=64)
-            nc.scalar.copy(
-                out=grouped[:].bitcast(F32).rearrange("p (c t u) -> p c t u", c=2, u=2),
-                in_=tom[:].rearrange("p c u t -> p c t u"),
-            )
-            grouped_tiles[pair] = grouped
-
-        def quantise(pair):
             if pair % 2 == 0:
-                codes_new = mx_pool.tile([P, HALF * P], U32, align_bytes=64)
-                scales_new = mx_pool.tile([P, HALF * P], U8, align_bytes=64)
-                mx_tiles[pair // 2] = (codes_new, scales_new)
-            codes, scales = mx_tiles[pair // 2]
-            cols = slice((pair % 2) * 2 * P, (pair % 2 + 1) * 2 * P)
-            nc.vector.quantize_mx(out=codes[:, cols].bitcast(FP8X4), scales=scales[:, cols], in_=grouped_tiles[pair][:])
+                grouped_new = grouped_pool.tile([P, HALF * P * PACK], BF16, align_bytes=64)
+                grouped_tiles[pair // 2] = grouped_new
+            grouped_words = grouped_tiles[pair // 2][:].bitcast(F32).rearrange("p (c t u) -> p c t u", c=HALF, u=2)
+            first = chunk_in_half(pair, 0)
+            nc.scalar.copy(out=grouped_words[:, first : first + 2, :, :], in_=tom[:].rearrange("p c u t -> p c t u"))
+
+        def quantise(half_batch):
+            codes = mx_pool.tile([P, HALF * P], U32, align_bytes=64)
+            scales = mx_pool.tile([P, HALF * P], U8, align_bytes=64)
+            nc.vector.quantize_mx(out=codes[:].bitcast(FP8X4), scales=scales[:], in_=grouped_tiles[half_batch][:])
+            mx_tiles[half_batch] = (codes, scales)
 
         def project(half_batch):
             codes, scales = mx_tiles[half_batch]
@@ -182,48 +187,41 @@ def tile_linearattention_pb_t_kernel(tc, q, k_sum, context, Wp, bp, out):
             out_by_token = out[b].rearrange("(p c) n -> p c n", c=CHUNKS)
             nc.sync.dma_start(out=out_by_token[:, half * HALF : (half + 1) * HALF, :], in_=out_sb[:])
 
-        for pair in range(2):
-            for quarter in range(BANKS_PER_PAIR):
-                transpose_queries(pair, quarter)
-
-        def run_round(r, waiting):
-            for bank in range(BANKS_PER_PAIR):
-                if bank == 2 and (r - PROJECT_LAG) % 2 == 0 and 0 <= r - PROJECT_LAG < PAIRS:
-                    project((r - PROJECT_LAG) // 2)
-                if bank == 2 and (r - PROJECT_LAG) % 2 == 1 and 0 <= r - PROJECT_LAG - 1 < PAIRS:
-                    store((r - PROJECT_LAG - 1) // 2)
-                filled = multiply(r, bank) if r < PAIRS else None
-                if waiting is not None:
-                    normalise(waiting, 0)
-                if filled is not None:
-                    invert(filled)
-                if waiting is not None:
-                    normalise(waiting, 1)
-                waiting = filled
+        def run_round(r):
+            for cc in range(2):
+                if cc == 1 and half_batch_due(r, PROJECT_LAG) is not None:
+                    project(half_batch_due(r, PROJECT_LAG))
+                if cc == 1 and half_batch_due(r, STORE_LAG) is not None:
+                    store(half_batch_due(r, STORE_LAG))
+                if r < PAIRS:
+                    attend(r, cc)
                 if r + 2 < PAIRS:
-                    transpose_queries(r + 2, bank)
+                    transpose_queries(r + 2, cc)
+            if r + 1 < PAIRS:
+                denominators(r + 1)
             if 0 <= r - 1 < PAIRS:
                 transpose_outputs(r - 1)
-            if 0 <= r - 2 < PAIRS:
-                quantise(r - 2)
-            return waiting
+            if half_batch_due(r, QUANTISE_LAG) is not None:
+                quantise(half_batch_due(r, QUANTISE_LAG))
 
-        waiting = None
+        for pair in range(2):
+            for cc in range(2):
+                transpose_queries(pair, cc)
+        denominators(0)
         for r in range(2):
-            waiting = run_round(r, waiting)
+            run_round(r)
 
-        wp_ps = psum.tile([P, 2, 2, P], F32, tag="bank")
+        wp_ps = psum.tile([P, 2, P], F32, tag="bank")
         wp_words = wp_rows[:].bitcast(F32)
         for u in range(2):
-            nc.tensor.transpose(wp_ps[:, 0, u, :], wp_words[:, u * P : (u + 1) * P], ident_f32[:])
+            nc.tensor.transpose(wp_ps[:, u, :], wp_words[:, u * P : (u + 1) * P], ident_f32[:])
         wp_grouped = consts.tile([P, DIM * PACK], BF16, align_bytes=64)
         nc.vector.tensor_copy(
-            out=wp_grouped[:].bitcast(F32).rearrange("p (n u) -> p n u", u=2),
-            in_=wp_ps[:, 0, :, :].rearrange("p u n -> p n u"),
+            out=wp_grouped[:].bitcast(F32).rearrange("p (n u) -> p n u", u=2), in_=wp_ps[:].rearrange("p u n -> p n u")
         )
         wp_codes = consts.tile([P, DIM], U32, align_bytes=64)
         wp_scales = consts.tile([P, DIM], U8, align_bytes=64)
         nc.vector.quantize_mx(out=wp_codes[:].bitcast(FP8X4), scales=wp_scales[:], in_=wp_grouped[:])
 
-        for r in range(2, PAIRS + PROJECT_LAG):
-            waiting = run_round(r, waiting)
+        for r in range(2, PAIRS + STORE_LAG - 1):
+            run_round(r)

@@ -122,13 +122,16 @@ def tile_linearattention_pb_t_kernel(tc, q, k_sum, context, Wp, bp, out):
             nc.vector.reciprocal(out=d_inv[:], in_=den[:])
             dinv_tiles[pair] = d_inv
 
-        def attend(pair, cc):
+        def multiply(pair, cc):
             b = pair // (CHUNKS // 2)
             prod = psum.tile([P, H, D], F32, tag="bank")
             for h in range(H):
                 nc.tensor.matmul(
                     out=prod[:, h, :], lhsT=qT_tiles[pair][:, cc, h, :], rhs=ctx[:, b * H + h, :], start=True, stop=True
                 )
+            return prod
+
+        def normalise(pair, cc, prod):
             if cc == 0:
                 om_new = om_pool.tile([P, 2, E], BF16)
                 om_tiles[pair] = om_new
@@ -188,17 +191,21 @@ def tile_linearattention_pb_t_kernel(tc, q, k_sum, context, Wp, bp, out):
             nc.sync.dma_start(out=out_by_token[:, half * HALF : (half + 1) * HALF, :], in_=out_sb[:])
 
         def run_round(r):
-            for cc in range(2):
-                if cc == 1 and half_batch_due(r, PROJECT_LAG) is not None:
-                    project(half_batch_due(r, PROJECT_LAG))
-                if cc == 1 and half_batch_due(r, STORE_LAG) is not None:
-                    store(half_batch_due(r, STORE_LAG))
-                if r < PAIRS:
-                    attend(r, cc)
-                if r + 2 < PAIRS:
-                    transpose_queries(r + 2, cc)
+            if r < PAIRS:
+                normalise(r, 0, multiply(r, 0))
+            if r + 2 < PAIRS:
+                transpose_queries(r + 2, 0)
+            if half_batch_due(r, PROJECT_LAG) is not None:
+                project(half_batch_due(r, PROJECT_LAG))
+            if half_batch_due(r, STORE_LAG) is not None:
+                store(half_batch_due(r, STORE_LAG))
+            prod = multiply(r, 1) if r < PAIRS else None
+            if r + 2 < PAIRS:
+                transpose_queries(r + 2, 1)
             if r + 1 < PAIRS:
                 denominators(r + 1)
+            if r < PAIRS:
+                normalise(r, 1, prod)
             if 0 <= r - 1 < PAIRS:
                 transpose_outputs(r - 1)
             if half_batch_due(r, QUANTISE_LAG) is not None:

@@ -17,22 +17,40 @@ DIM = 128
 E = H * D
 P = 128
 PACK = 4
+WORD_BLOCKS = 2
 CHUNKS = T // P
+PAIR = 2
 HALF = CHUNKS // 2
+PAIRS_PER_BATCH = CHUNKS // PAIR
+PAIRS_PER_HALF = HALF // PAIR
 HALVES = 2 * B
-PAIRS = 2 * HALVES
+PAIRS = B * PAIRS_PER_BATCH
+BIAS_ROW = B * H
 PSUM_BANKS = 8
+
+TRANSPOSE_LEAD = 2
+LOAD_LEAD = 4
+ROUNDS_BEFORE_WP = 2
 QUANTISE_LAG = 3
 PROJECT_LAG = 5
 STORE_LAG = 6
+
+QT_BUFS = 4
+DINV_BUFS = 4
+OM_BUFS = 4
+GROUPED_BUFS = 3
+MX_BUFS = 3
+REST_BUFS = 3
+OUT_BUFS = 4
+Q_BUFS = 8
 
 FLOPS = 2 * B * H * T * D * D + 2 * B * T * E * DIM
 
 
 def half_batch_due(r, lag):
     first_round = r - lag
-    if first_round % 2 == 0 and 0 <= first_round < PAIRS:
-        return first_round // 2
+    if first_round % PAIRS_PER_HALF == 0 and 0 <= first_round < PAIRS:
+        return first_round // PAIRS_PER_HALF
     return None
 
 
@@ -40,35 +58,39 @@ def tile_linearattention_pb_t_kernel(tc, q, k_sum, context, Wp, bp, out):
     nc = tc.nc
     with ExitStack() as stack:
         consts = stack.enter_context(tc.tile_pool(name="consts", bufs=1))
-        q_pool = stack.enter_context(tc.tile_pool(name="q", bufs=HALVES))
-        qT_pool = stack.enter_context(tc.tile_pool(name="qT", bufs=4))
-        dinv_pool = stack.enter_context(tc.tile_pool(name="dinv", bufs=4))
-        om_pool = stack.enter_context(tc.tile_pool(name="om", bufs=4))
-        grouped_pool = stack.enter_context(tc.tile_pool(name="grouped", bufs=3))
-        mx_pool = stack.enter_context(tc.tile_pool(name="mx", bufs=3))
-        resT_pool = stack.enter_context(tc.tile_pool(name="resT", bufs=3))
-        out_pool = stack.enter_context(tc.tile_pool(name="out", bufs=8))
+        q_pool = stack.enter_context(tc.tile_pool(name="q", bufs=Q_BUFS))
+        qT_pool = stack.enter_context(tc.tile_pool(name="qT", bufs=QT_BUFS))
+        dinv_pool = stack.enter_context(tc.tile_pool(name="dinv", bufs=DINV_BUFS))
+        om_pool = stack.enter_context(tc.tile_pool(name="om", bufs=OM_BUFS))
+        grouped_pool = stack.enter_context(tc.tile_pool(name="grouped", bufs=GROUPED_BUFS))
+        mx_pool = stack.enter_context(tc.tile_pool(name="mx", bufs=MX_BUFS))
+        resT_pool = stack.enter_context(tc.tile_pool(name="resT", bufs=REST_BUFS))
+        out_pool = stack.enter_context(tc.tile_pool(name="out", bufs=OUT_BUFS))
         psum = stack.enter_context(tc.psum_pool(name="psum", bufs=PSUM_BANKS))
         stack.enter_context(tc.manual_schedule())
 
         small_rows = consts.tile([P, D], BF16)
         nc.vector.memset(small_rows[:], 0.0)
-        nc.sync.dma_start(out=small_rows[0 : B * H, :], in_=k_sum.rearrange("b h o d -> (b h o) d"))
-        nc.sync.dma_start(out=small_rows[B * H : B * H + 1, :], in_=bp.rearrange("(o n) -> o n", o=1))
+        nc.sync.dma_start(out=small_rows[0:BIAS_ROW, :], in_=k_sum.rearrange("b h o d -> (b h o) d"))
+        nc.sync.dma_start(out=small_rows[BIAS_ROW : BIAS_ROW + 1, :], in_=bp.rearrange("(o n) -> o n", o=1))
         wp_rows = consts.tile([P, E], BF16)
         ctx = consts.tile([P, B * H, D], BF16)
-        q_tiles = []
+        q_tiles = {}
         context_by_feature = context.rearrange("b h d e -> d (b h) e")
-        for b in range(B):
+
+        def load(half_batch):
+            b, half = divmod(half_batch, 2)
             q_by_token = q[b].rearrange("h (p c) d -> p h c d", c=CHUNKS)
-            for half in range(2):
-                q_half = q_pool.tile([P, H, HALF, D], BF16)
-                nc.sync.dma_start(out=q_half[:], in_=q_by_token[:, :, half * HALF : (half + 1) * HALF, :])
-                q_tiles.append(q_half)
-                if half == 0:
-                    heads = slice(b * H, (b + 1) * H)
-                    nc.sync.dma_start(out=ctx[:, heads, :], in_=context_by_feature[:, heads, :])
-            if b == 0:
+            q_half = q_pool.tile([P, H, HALF, D], BF16)
+            nc.sync.dma_start(out=q_half[:], in_=q_by_token[:, :, half * HALF : (half + 1) * HALF, :])
+            q_tiles[half_batch] = q_half
+            if half == 0:
+                heads = slice(b * H, (b + 1) * H)
+                nc.sync.dma_start(out=ctx[:, heads, :], in_=context_by_feature[:, heads, :])
+
+        for half_batch in range(LOAD_LEAD):
+            load(half_batch)
+            if half_batch == 1:
                 nc.sync.dma_start(out=wp_rows[:], in_=Wp)
 
         ident_bf16 = consts.tile([P, P], BF16)
@@ -79,9 +101,9 @@ def tile_linearattention_pb_t_kernel(tc, q, k_sum, context, Wp, bp, out):
         small_ps = psum.tile([P, P], BF16, tag="bank")
         nc.tensor.transpose(small_ps[:], small_rows[:], ident_bf16[:])
         ksumT = consts.tile([P, B * H], BF16)
-        nc.vector.tensor_copy(out=ksumT[:], in_=small_ps[:, 0 : B * H])
+        nc.vector.tensor_copy(out=ksumT[:], in_=small_ps[:, 0:BIAS_ROW])
         bias = consts.tile([P, 1], F32)
-        nc.vector.tensor_copy(out=bias[:], in_=small_ps[:, B * H : B * H + 1])
+        nc.vector.tensor_copy(out=bias[:], in_=small_ps[:, BIAS_ROW : BIAS_ROW + 1])
 
         tq_tiles = {}
         qT_tiles = {}
@@ -92,24 +114,26 @@ def tile_linearattention_pb_t_kernel(tc, q, k_sum, context, Wp, bp, out):
         resT_tiles = {}
 
         def chunk_in_half(pair, cc):
-            return 2 * (pair % 2) + cc
+            return PAIR * (pair % PAIRS_PER_HALF) + cc
 
         def transpose_queries(pair, cc):
             if cc == 0:
-                tq_new = psum.tile([P, 2, H, P], BF16, tag="bank")
+                tq_new = psum.tile([P, PAIR, H, P], BF16, tag="bank")
                 tq_tiles[pair] = tq_new
             tq = tq_tiles[pair]
             for h in range(H):
-                nc.tensor.transpose(tq[:, cc, h, :], q_tiles[pair // 2][:, h, chunk_in_half(pair, cc), :], ident_bf16[:])
-            if cc == 1:
-                qT = qT_pool.tile([P, 2, H, P], BF16)
+                nc.tensor.transpose(
+                    tq[:, cc, h, :], q_tiles[pair // PAIRS_PER_HALF][:, h, chunk_in_half(pair, cc), :], ident_bf16[:]
+                )
+            if cc == PAIR - 1:
+                qT = qT_pool.tile([P, PAIR, H, P], BF16)
                 nc.scalar.copy(out=qT[:], in_=tq[:])
                 qT_tiles[pair] = qT
 
         def denominators(pair):
-            b = pair // (CHUNKS // 2)
-            den = psum.tile([P, 2, H], F32, tag="bank")
-            for cc in range(2):
+            b = pair // PAIRS_PER_BATCH
+            den = psum.tile([P, PAIR, H], F32, tag="bank")
+            for cc in range(PAIR):
                 for h in range(H):
                     nc.tensor.matmul(
                         out=den[:, cc, h : h + 1],
@@ -118,12 +142,12 @@ def tile_linearattention_pb_t_kernel(tc, q, k_sum, context, Wp, bp, out):
                         start=True,
                         stop=True,
                     )
-            d_inv = dinv_pool.tile([P, 2, H], F32)
+            d_inv = dinv_pool.tile([P, PAIR, H], F32)
             nc.vector.reciprocal(out=d_inv[:], in_=den[:])
             dinv_tiles[pair] = d_inv
 
         def multiply(pair, cc):
-            b = pair // (CHUNKS // 2)
+            b = pair // PAIRS_PER_BATCH
             prod = psum.tile([P, H, D], F32, tag="bank")
             for h in range(H):
                 nc.tensor.matmul(
@@ -133,30 +157,34 @@ def tile_linearattention_pb_t_kernel(tc, q, k_sum, context, Wp, bp, out):
 
         def normalise(pair, cc, prod):
             if cc == 0:
-                om_new = om_pool.tile([P, 2, E], BF16)
+                om_new = om_pool.tile([P, PAIR, E], BF16)
                 om_tiles[pair] = om_new
             for h in range(H):
                 nc.vector.scalar_tensor_tensor(
                     out=om_tiles[pair][:, cc, h * D : (h + 1) * D],
                     in0=prod[:, h, :],
                     scalar=dinv_tiles[pair][:, cc, h : h + 1],
-                    in1=q_tiles[pair // 2][:, h, chunk_in_half(pair, cc), :],
+                    in1=q_tiles[pair // PAIRS_PER_HALF][:, h, chunk_in_half(pair, cc), :],
                     op0=MULT,
                     op1=ADD,
                 )
 
         def transpose_outputs(pair):
             om_words = om_tiles[pair][:].bitcast(F32)
-            tom = psum.tile([P, 2, 2, P], F32, tag="bank")
-            for cc in range(2):
-                for u in range(2):
+            tom = psum.tile([P, PAIR, WORD_BLOCKS, P], F32, tag="bank")
+            for cc in range(PAIR):
+                for u in range(WORD_BLOCKS):
                     nc.tensor.transpose(tom[:, cc, u, :], om_words[:, cc, u * P : (u + 1) * P], ident_f32[:])
-            if pair % 2 == 0:
+            if pair % PAIRS_PER_HALF == 0:
                 grouped_new = grouped_pool.tile([P, HALF * P * PACK], BF16, align_bytes=64)
-                grouped_tiles[pair // 2] = grouped_new
-            grouped_words = grouped_tiles[pair // 2][:].bitcast(F32).rearrange("p (c t u) -> p c t u", c=HALF, u=2)
+                grouped_tiles[pair // PAIRS_PER_HALF] = grouped_new
+            grouped_words = (
+                grouped_tiles[pair // PAIRS_PER_HALF][:]
+                .bitcast(F32)
+                .rearrange("p (c t u) -> p c t u", c=HALF, u=WORD_BLOCKS)
+            )
             first = chunk_in_half(pair, 0)
-            nc.scalar.copy(out=grouped_words[:, first : first + 2, :, :], in_=tom[:].rearrange("p c u t -> p c t u"))
+            nc.scalar.copy(out=grouped_words[:, first : first + PAIR, :, :], in_=tom[:].rearrange("p c u t -> p c t u"))
 
         def quantise(half_batch):
             codes = mx_pool.tile([P, HALF * P], U32, align_bytes=64)
@@ -191,17 +219,19 @@ def tile_linearattention_pb_t_kernel(tc, q, k_sum, context, Wp, bp, out):
             nc.sync.dma_start(out=out_by_token[:, half * HALF : (half + 1) * HALF, :], in_=out_sb[:])
 
         def run_round(r):
+            if r % PAIRS_PER_HALF == 0 and r // PAIRS_PER_HALF + LOAD_LEAD < HALVES:
+                load(r // PAIRS_PER_HALF + LOAD_LEAD)
             if r < PAIRS:
                 normalise(r, 0, multiply(r, 0))
-            if r + 2 < PAIRS:
-                transpose_queries(r + 2, 0)
+            if r + TRANSPOSE_LEAD < PAIRS:
+                transpose_queries(r + TRANSPOSE_LEAD, 0)
             if half_batch_due(r, PROJECT_LAG) is not None:
                 project(half_batch_due(r, PROJECT_LAG))
             if half_batch_due(r, STORE_LAG) is not None:
                 store(half_batch_due(r, STORE_LAG))
             prod = multiply(r, 1) if r < PAIRS else None
-            if r + 2 < PAIRS:
-                transpose_queries(r + 2, 1)
+            if r + TRANSPOSE_LEAD < PAIRS:
+                transpose_queries(r + TRANSPOSE_LEAD, 1)
             if r + 1 < PAIRS:
                 denominators(r + 1)
             if r < PAIRS:
@@ -211,24 +241,25 @@ def tile_linearattention_pb_t_kernel(tc, q, k_sum, context, Wp, bp, out):
             if half_batch_due(r, QUANTISE_LAG) is not None:
                 quantise(half_batch_due(r, QUANTISE_LAG))
 
-        for pair in range(2):
-            for cc in range(2):
+        for pair in range(TRANSPOSE_LEAD):
+            for cc in range(PAIR):
                 transpose_queries(pair, cc)
         denominators(0)
-        for r in range(2):
+        for r in range(ROUNDS_BEFORE_WP):
             run_round(r)
 
-        wp_ps = psum.tile([P, 2, P], F32, tag="bank")
+        wp_ps = psum.tile([P, WORD_BLOCKS, P], F32, tag="bank")
         wp_words = wp_rows[:].bitcast(F32)
-        for u in range(2):
+        for u in range(WORD_BLOCKS):
             nc.tensor.transpose(wp_ps[:, u, :], wp_words[:, u * P : (u + 1) * P], ident_f32[:])
         wp_grouped = consts.tile([P, DIM * PACK], BF16, align_bytes=64)
         nc.vector.tensor_copy(
-            out=wp_grouped[:].bitcast(F32).rearrange("p (n u) -> p n u", u=2), in_=wp_ps[:].rearrange("p u n -> p n u")
+            out=wp_grouped[:].bitcast(F32).rearrange("p (n u) -> p n u", u=WORD_BLOCKS),
+            in_=wp_ps[:].rearrange("p u n -> p n u"),
         )
         wp_codes = consts.tile([P, DIM], U32, align_bytes=64)
         wp_scales = consts.tile([P, DIM], U8, align_bytes=64)
         nc.vector.quantize_mx(out=wp_codes[:].bitcast(FP8X4), scales=wp_scales[:], in_=wp_grouped[:])
 
-        for r in range(2, PAIRS + STORE_LAG - 1):
+        for r in range(ROUNDS_BEFORE_WP, PAIRS - PAIRS_PER_HALF + STORE_LAG + 1):
             run_round(r)

@@ -29,8 +29,6 @@ BIAS_ROW = B * H
 PSUM_BANKS = 8
 
 TRANSPOSE_LEAD = 2
-LOAD_LEAD = 4
-ROUNDS_BEFORE_WP = 2
 QUANTISE_LAG = 3
 PROJECT_LAG = 5
 STORE_LAG = 6
@@ -41,8 +39,7 @@ OM_BUFS = 4
 GROUPED_BUFS = 3
 MX_BUFS = 3
 REST_BUFS = 3
-OUT_BUFS = 4
-Q_BUFS = 8
+OUT_BUFS = 16
 
 FLOPS = 2 * B * H * T * D * D + 2 * B * T * E * DIM
 
@@ -58,7 +55,7 @@ def tile_linearattention_pb_t_kernel(tc, q, k_sum, context, Wp, bp, out):
     nc = tc.nc
     with ExitStack() as stack:
         consts = stack.enter_context(tc.tile_pool(name="consts", bufs=1))
-        q_pool = stack.enter_context(tc.tile_pool(name="q", bufs=Q_BUFS))
+        q_pool = stack.enter_context(tc.tile_pool(name="q", bufs=HALVES))
         qT_pool = stack.enter_context(tc.tile_pool(name="qT", bufs=QT_BUFS))
         dinv_pool = stack.enter_context(tc.tile_pool(name="dinv", bufs=DINV_BUFS))
         om_pool = stack.enter_context(tc.tile_pool(name="om", bufs=OM_BUFS))
@@ -75,22 +72,18 @@ def tile_linearattention_pb_t_kernel(tc, q, k_sum, context, Wp, bp, out):
         nc.sync.dma_start(out=small_rows[BIAS_ROW : BIAS_ROW + 1, :], in_=bp.rearrange("(o n) -> o n", o=1))
         wp_rows = consts.tile([P, E], BF16)
         ctx = consts.tile([P, B * H, D], BF16)
-        q_tiles = {}
+        q_tiles = []
         context_by_feature = context.rearrange("b h d e -> d (b h) e")
-
-        def load(half_batch):
-            b, half = divmod(half_batch, 2)
+        for b in range(B):
             q_by_token = q[b].rearrange("h (p c) d -> p h c d", c=CHUNKS)
-            q_half = q_pool.tile([P, H, HALF, D], BF16)
-            nc.sync.dma_start(out=q_half[:], in_=q_by_token[:, :, half * HALF : (half + 1) * HALF, :])
-            q_tiles[half_batch] = q_half
-            if half == 0:
-                heads = slice(b * H, (b + 1) * H)
-                nc.sync.dma_start(out=ctx[:, heads, :], in_=context_by_feature[:, heads, :])
-
-        for half_batch in range(LOAD_LEAD):
-            load(half_batch)
-            if half_batch == 1:
+            for half in range(2):
+                q_half = q_pool.tile([P, H, HALF, D], BF16)
+                nc.sync.dma_start(out=q_half[:], in_=q_by_token[:, :, half * HALF : (half + 1) * HALF, :])
+                q_tiles.append(q_half)
+                if half == 0:
+                    heads = slice(b * H, (b + 1) * H)
+                    nc.sync.dma_start(out=ctx[:, heads, :], in_=context_by_feature[:, heads, :])
+            if b == 0:
                 nc.sync.dma_start(out=wp_rows[:], in_=Wp)
 
         ident_bf16 = consts.tile([P, P], BF16)
@@ -219,8 +212,6 @@ def tile_linearattention_pb_t_kernel(tc, q, k_sum, context, Wp, bp, out):
             nc.sync.dma_start(out=out_by_token[:, half * HALF : (half + 1) * HALF, :], in_=out_sb[:])
 
         def run_round(r):
-            if r % PAIRS_PER_HALF == 0 and r // PAIRS_PER_HALF + LOAD_LEAD < HALVES:
-                load(r // PAIRS_PER_HALF + LOAD_LEAD)
             if r < PAIRS:
                 normalise(r, 0, multiply(r, 0))
             if r + TRANSPOSE_LEAD < PAIRS:
@@ -245,7 +236,7 @@ def tile_linearattention_pb_t_kernel(tc, q, k_sum, context, Wp, bp, out):
             for cc in range(PAIR):
                 transpose_queries(pair, cc)
         denominators(0)
-        for r in range(ROUNDS_BEFORE_WP):
+        for r in range(2):
             run_round(r)
 
         wp_ps = psum.tile([P, WORD_BLOCKS, P], F32, tag="bank")
@@ -261,5 +252,5 @@ def tile_linearattention_pb_t_kernel(tc, q, k_sum, context, Wp, bp, out):
         wp_scales = consts.tile([P, DIM], U8, align_bytes=64)
         nc.vector.quantize_mx(out=wp_codes[:].bitcast(FP8X4), scales=wp_scales[:], in_=wp_grouped[:])
 
-        for r in range(ROUNDS_BEFORE_WP, PAIRS - PAIRS_PER_HALF + STORE_LAG + 1):
+        for r in range(2, PAIRS - PAIRS_PER_HALF + STORE_LAG + 1):
             run_round(r)

from contextlib import ExitStack

import concourse.mybir as mybir
from concourse.masks import make_identity

BF16 = mybir.dt.bfloat16
F32 = mybir.dt.float32
U32 = mybir.dt.uint32
U8 = mybir.dt.uint8
FP8X4 = mybir.dt.float8_e4m3fn_x4
IDENTITY = mybir.ActivationFunctionType.Identity
MULT = mybir.AluOpType.mult
ADD = mybir.AluOpType.add

B, H, T, D = 16, 4, 1024, 128
DIM = 128
E = H * D
P = 128
PACK = 4
WORD_BLOCKS = 2
CHUNKS = T // P
PAIR = 2
HALF = CHUNKS // 2
PAIRS_PER_BATCH = CHUNKS // PAIR
PAIRS_PER_HALF = HALF // PAIR
HALVES = 2 * B
PAIRS = B * PAIRS_PER_BATCH
BIAS_ROW = B * H
PSUM_BANKS = 8

TRANSPOSE_LEAD = 2
QUANTISE_LAG = 3
PROJECT_LAG = 5
STORE_LAG = 6

QT_BUFS = 4
DINV_BUFS = 4
OM_BUFS = 4
GROUPED_BUFS = 3
MX_BUFS = 3
REST_BUFS = 3
OUT_BUFS = 16

FLOPS = 2 * B * H * T * D * D + 2 * B * T * E * DIM


def half_batch_due(r, lag):
    first_round = r - lag
    if first_round % PAIRS_PER_HALF == 0 and 0 <= first_round < PAIRS:
        return first_round // PAIRS_PER_HALF
    return None


def tile_linearattention_pb_t_kernel(tc, q, k_sum, context, Wp, bp, out):
    nc = tc.nc
    with ExitStack() as stack:
        consts = stack.enter_context(tc.tile_pool(name="consts", bufs=1))
        q_pool = stack.enter_context(tc.tile_pool(name="q", bufs=HALVES))
        qT_pool = stack.enter_context(tc.tile_pool(name="qT", bufs=QT_BUFS))
        dinv_pool = stack.enter_context(tc.tile_pool(name="dinv", bufs=DINV_BUFS))
        om_pool = stack.enter_context(tc.tile_pool(name="om", bufs=OM_BUFS))
        grouped_pool = stack.enter_context(tc.tile_pool(name="grouped", bufs=GROUPED_BUFS))
        mx_pool = stack.enter_context(tc.tile_pool(name="mx", bufs=MX_BUFS))
        resT_pool = stack.enter_context(tc.tile_pool(name="resT", bufs=REST_BUFS))
        out_pool = stack.enter_context(tc.tile_pool(name="out", bufs=OUT_BUFS))
        psum = stack.enter_context(tc.psum_pool(name="psum", bufs=PSUM_BANKS))
        stack.enter_context(tc.manual_schedule())

        small_rows = consts.tile([P, D], BF16)
        nc.vector.memset(small_rows[:], 0.0)
        nc.sync.dma_start(out=small_rows[0:BIAS_ROW, :], in_=k_sum.rearrange("b h o d -> (b h o) d"))
        nc.sync.dma_start(out=small_rows[BIAS_ROW : BIAS_ROW + 1, :], in_=bp.rearrange("(o n) -> o n", o=1))
        wp_rows = consts.tile([P, E], BF16)
        ctx = consts.tile([P, B * H, D], BF16)
        q_tiles = []
        context_by_feature = context.rearrange("b h d e -> d (b h) e")
        for b in range(B):
            q_by_token = q[b].rearrange("h (p c) d -> p h c d", c=CHUNKS)
            for half in range(2):
                q_half = q_pool.tile([P, H, HALF, D], BF16)
                nc.sync.dma_start(out=q_half[:], in_=q_by_token[:, :, half * HALF : (half + 1) * HALF, :])
                q_tiles.append(q_half)
                if half == 0:
                    heads = slice(b * H, (b + 1) * H)
                    nc.sync.dma_start(out=ctx[:, heads, :], in_=context_by_feature[:, heads, :])
            if b == 0:
                nc.sync.dma_start(out=wp_rows[:], in_=Wp)

        ident_bf16 = consts.tile([P, P], BF16)
        make_identity(nc, ident_bf16[:])
        ident_f32 = consts.tile([P, P], F32)
        make_identity(nc, ident_f32[:])

        small_ps = psum.tile([P, P], BF16, tag="bank")
        nc.tensor.transpose(small_ps[:], small_rows[:], ident_bf16[:])
        ksumT = consts.tile([P, B * H], BF16)
        nc.vector.tensor_copy(out=ksumT[:], in_=small_ps[:, 0:BIAS_ROW])
        bias = consts.tile([P, 1], F32)
        nc.vector.tensor_copy(out=bias[:], in_=small_ps[:, BIAS_ROW : BIAS_ROW + 1])

        tq_tiles = {}
        qT_tiles = {}
        dinv_tiles = {}
        om_tiles = {}
        grouped_tiles = {}
        mx_tiles = {}
        resT_tiles = {}

        def chunk_in_half(pair, cc):
            return PAIR * (pair % PAIRS_PER_HALF) + cc

        def transpose_queries(pair, cc):
            if cc == 0:
                tq_new = psum.tile([P, PAIR, H, P], BF16, tag="bank")
                tq_tiles[pair] = tq_new
            tq = tq_tiles[pair]
            for h in range(H):
                nc.tensor.transpose(
                    tq[:, cc, h, :], q_tiles[pair // PAIRS_PER_HALF][:, h, chunk_in_half(pair, cc), :], ident_bf16[:]
                )
            if cc == PAIR - 1:
                qT = qT_pool.tile([P, PAIR, H, P], BF16)
                nc.scalar.copy(out=qT[:], in_=tq[:])
                qT_tiles[pair] = qT

        def denominators(pair):
            b = pair // PAIRS_PER_BATCH
            den = psum.tile([P, PAIR, H], F32, tag="bank")
            for cc in range(PAIR):
                for h in range(H):
                    nc.tensor.matmul(
                        out=den[:, cc, h : h + 1],
                        lhsT=qT_tiles[pair][:, cc, h, :],
                        rhs=ksumT[:, b * H + h : b * H + h + 1],
                        start=True,
                        stop=True,
                    )
            d_inv = dinv_pool.tile([P, PAIR, H], F32)
            nc.vector.reciprocal(out=d_inv[:], in_=den[:])
            dinv_tiles[pair] = d_inv

        def multiply(pair, cc):
            b = pair // PAIRS_PER_BATCH
            prod = psum.tile([P, H, D], F32, tag="bank")
            for h in range(H):
                nc.tensor.matmul(
                    out=prod[:, h, :], lhsT=qT_tiles[pair][:, cc, h, :], rhs=ctx[:, b * H + h, :], start=True, stop=True
                )
            return prod

        def normalise(pair, cc, prod):
            if cc == 0:
                om_new = om_pool.tile([P, PAIR, E], BF16)
                om_tiles[pair] = om_new
            for h in range(H):
                nc.vector.scalar_tensor_tensor(
                    out=om_tiles[pair][:, cc, h * D : (h + 1) * D],
                    in0=prod[:, h, :],
                    scalar=dinv_tiles[pair][:, cc, h : h + 1],
                    in1=q_tiles[pair // PAIRS_PER_HALF][:, h, chunk_in_half(pair, cc), :],
                    op0=MULT,
                    op1=ADD,
                )

        def transpose_outputs(pair):
            om_words = om_tiles[pair][:].bitcast(F32)
            tom = psum.tile([P, PAIR, WORD_BLOCKS, P], F32, tag="bank")
            for cc in range(PAIR):
                for u in range(WORD_BLOCKS):
                    nc.tensor.transpose(tom[:, cc, u, :], om_words[:, cc, u * P : (u + 1) * P], ident_f32[:])
            if pair % PAIRS_PER_HALF == 0:
                grouped_new = grouped_pool.tile([P, HALF * P * PACK], BF16, align_bytes=64)
                grouped_tiles[pair // PAIRS_PER_HALF] = grouped_new
            grouped_words = (
                grouped_tiles[pair // PAIRS_PER_HALF][:]
                .bitcast(F32)
                .rearrange("p (c t u) -> p c t u", c=HALF, u=WORD_BLOCKS)
            )
            first = chunk_in_half(pair, 0)
            nc.scalar.copy(out=grouped_words[:, first : first + PAIR, :, :], in_=tom[:].rearrange("p c u t -> p c t u"))

        def quantise(half_batch):
            codes = mx_pool.tile([P, HALF * P], U32, align_bytes=64)
            scales = mx_pool.tile([P, HALF * P], U8, align_bytes=64)
            nc.vector.quantize_mx(out=codes[:].bitcast(FP8X4), scales=scales[:], in_=grouped_tiles[half_batch][:])
            mx_tiles[half_batch] = (codes, scales)

        def project(half_batch):
            codes, scales = mx_tiles[half_batch]
            resT = psum.tile([P, HALF * P], F32, tag="bank")
            nc.tensor.matmul_mx(
                out=resT[:],
                lhsT=wp_codes[:].bitcast(FP8X4),
                lhsT_scale=wp_scales[:],
                rhs=codes[:].bitcast(FP8X4),
                rhs_scale=scales[:],
                start=True,
                stop=True,
            )
            resT_sb = resT_pool.tile([P, HALF * P], F32)
            nc.scalar.activation(out=resT_sb[:], in_=resT[:], func=IDENTITY, bias=bias[:, 0:1], scale=1.0)
            resT_tiles[half_batch] = resT_sb

        def store(half_batch):
            res = psum.tile([P, HALF, DIM], F32, tag="bank")
            for c in range(HALF):
                nc.tensor.transpose(res[:, c, :], resT_tiles[half_batch][:, c * P : (c + 1) * P], ident_f32[:])
            out_sb = out_pool.tile([P, HALF, DIM], F32)
            nc.scalar.copy(out=out_sb[:], in_=res[:])
            b, half = divmod(half_batch, 2)
            out_by_token = out[b].rearrange("(p c) n -> p c n", c=CHUNKS)
            nc.sync.dma_start(out=out_by_token[:, half * HALF : (half + 1) * HALF, :], in_=out_sb[:])

        def run_round(r):
            if r < PAIRS:
                normalise(r, 0, multiply(r, 0))
            if r + TRANSPOSE_LEAD < PAIRS:
                transpose_queries(r + TRANSPOSE_LEAD, 0)
            if half_batch_due(r, PROJECT_LAG) is not None:
                project(half_batch_due(r, PROJECT_LAG))
            if half_batch_due(r, STORE_LAG) is not None:
                store(half_batch_due(r, STORE_LAG))
            prod = multiply(r, 1) if r < PAIRS else None
            if r + TRANSPOSE_LEAD < PAIRS:
                transpose_queries(r + TRANSPOSE_LEAD, 1)
            if r + 1 < PAIRS:
                denominators(r + 1)
            if r < PAIRS:
                normalise(r, 1, prod)
            if 0 <= r - 1 < PAIRS:
                transpose_outputs(r - 1)
            if half_batch_due(r, QUANTISE_LAG) is not None:
                quantise(half_batch_due(r, QUANTISE_LAG))

        for pair in range(TRANSPOSE_LEAD):
            for cc in range(PAIR):
                transpose_queries(pair, cc)
        denominators(0)
        for r in range(2):
            run_round(r)

        wp_ps = psum.tile([P, WORD_BLOCKS, P], F32, tag="bank")
        wp_words = wp_rows[:].bitcast(F32)
        for u in range(WORD_BLOCKS):
            nc.tensor.transpose(wp_ps[:, u, :], wp_words[:, u * P : (u + 1) * P], ident_f32[:])
        wp_grouped = consts.tile([P, DIM * PACK], BF16, align_bytes=64)
        nc.vector.tensor_copy(
            out=wp_grouped[:].bitcast(F32).rearrange("p (n u) -> p n u", u=WORD_BLOCKS),
            in_=wp_ps[:].rearrange("p u n -> p n u"),
        )
        wp_codes = consts.tile([P, DIM], U32, align_bytes=64)
        wp_scales = consts.tile([P, DIM], U8, align_bytes=64)
        nc.vector.quantize_mx(out=wp_codes[:].bitcast(FP8X4), scales=wp_scales[:], in_=wp_grouped[:])

        for r in range(2, PAIRS - PAIRS_PER_HALF + STORE_LAG + 1):
            run_round(r)
